import numpy as np
import ml_dtypes


def mxq(x, axis, fmt="e4m3"):
    dtype, down = {"e4m3": (ml_dtypes.float8_e4m3fn, 7), "e5m2": (ml_dtypes.float8_e5m2, 14)}[fmt]
    v = np.moveaxis(np.asarray(x, np.float32).astype(ml_dtypes.bfloat16).astype(np.float64), axis, -1)
    blocks = v.reshape(v.shape[:-1] + (-1, 32))
    amax = np.abs(blocks).max(-1, keepdims=True)
    byte = np.maximum(np.where(amax > 0, np.frexp(amax)[1] - 1 + 127, 0) - down, 1)
    scale = np.exp2(byte - 127.0)
    codes = (blocks / scale).astype(np.float32).astype(dtype).astype(np.float64)
    return np.moveaxis((codes * scale).reshape(v.shape), -1, axis)


WIDE = False


def mx_kscale(k):
    if not WIDE:
        return np.ones(k)
    levels = np.array([10, -10, 5, -5, 0])
    a = np.random.permutation(np.resize(levels, k // 512 * 4)).reshape(k // 512, 4)
    idx = np.arange(k)
    return np.exp2(a[idx // 512, idx % 128 // 32])


BF16 = ml_dtypes.bfloat16


def bf(x):
    return np.asarray(x, np.float32).astype(BF16)


def f64(x):
    return np.asarray(x).astype(np.float64)


B, N, D, L = 4, 1024, 512, 3
GAIN = 8.0


def setup_inputs():
    s, t = mx_kscale(N), mx_kscale(D)
    c = np.exp2(np.round(np.log2(np.mean(1.0 / s))))
    sc = s * c
    deg = np.exp2(np.random.uniform(-1.0, 2.0, (B, N, 1)))
    adj = deg * np.exp(2.0 * np.random.standard_normal((B, N, N)) - 2.0) / N
    return {"x": bf(np.random.standard_normal((B, N, D)) * sc[:, None] * t),
            "adj": bf(adj / sc),
            "w": bf(np.random.standard_normal((D, D)) * GAIN / np.sqrt(D) / t[:, None]),
            "b": bf(np.random.standard_normal(D) * 0.5)}


def reference(x, adj, w, b):
    a = f64(adj)
    denom = a.sum(axis=2, keepdims=True) + 1.0
    ax = mxq(a, 2, "e4m3") @ mxq(f64(x), 1, "e4m3")
    axw = (mxq(ax, 2, "e4m3") @ mxq(f64(w), 0, "e4m3")) + f64(b)
    return np.maximum(axw / denom, 0.0)

@@ -1,0 +1,311 @@
+from contextlib import ExitStack
+
+import concourse.mybir as mybir
+from concourse.masks import make_identity
+
+F32 = mybir.dt.float32
+BF16 = mybir.dt.bfloat16
+U32 = mybir.dt.uint32
+U8 = mybir.dt.uint8
+FP8X4 = mybir.dt.float8_e4m3fn_x4
+ALU = mybir.AluOpType
+ACT = mybir.ActivationFunctionType
+AX = mybir.AxisListType
+
+G = 4
+N = 1024
+D = 512
+P = 128
+R = N // P
+NU = G * R
+NPAIR = NU // 2
+FLOPS = 2 * G * N * N * D + 2 * G * N * D * D
+
+MANUAL = True
+C2_ON_V = ()
+B_ON_V = ()
+
+
+def tile_msamodel_pa_kernel(tc, x, adj, w, b, out):
+    nc = tc.nc
+    with ExitStack() as ctx:
+        const = ctx.enter_context(tc.tile_pool(name="const", bufs=1))
+        two = ctx.enter_context(tc.tile_pool(name="two", bufs=2))
+        four = ctx.enter_context(tc.tile_pool(name="four", bufs=4))
+        six = ctx.enter_context(tc.tile_pool(name="six", bufs=6))
+        ps_tp = ctx.enter_context(tc.psum_pool(name="ps_tp", bufs=2))
+        ps_p1 = ctx.enter_context(tc.psum_pool(name="ps_p1", bufs=3))
+        ps_p2 = ctx.enter_context(tc.psum_pool(name="ps_p2", bufs=2))
+        ps_pd = ctx.enter_context(tc.psum_pool(name="ps_pd", bufs=1))
+        if MANUAL:
+            ctx.enter_context(tc.manual_schedule())
+
+        adj_v = adj.rearrange("g (p r) j -> g p (r j)", r=R)
+        x_v = x.rearrange("g (k p e) d -> g p k (e d)", k=4, p=P, e=2)
+        out_v = out.rearrange("g (p r) e -> g p (r e)", r=R)
+
+        adj_sb = [const.tile([P, R * N], BF16, name="adj%d" % g) for g in range(G)]
+        adj_w = [t[:].bitcast(F32) for t in adj_sb]
+        x_sb = [const.tile([P, 4 * N], BF16, name="x%d" % g) for g in range(G)]
+        w_sb = const.tile([P, 4 * D], BF16, name="w_sb")
+        wg = const.tile([P, 4 * D], BF16, name="wg", align_bytes=64)
+        wc = const.tile([P, D], U32, name="wc", align_bytes=64)
+        ws = const.tile([P, D], U8, name="ws", align_bytes=64)
+        zb = const.tile([P, D], BF16, name="zb")
+        ones = const.tile([P, P], BF16, name="ones")
+        identf = const.tile([P, P], F32, name="identf")
+        identb = const.tile([P, P], BF16, name="identb")
+        bb = const.tile([P, D], F32, name="bb")
+        junk = const.tile([P, N], BF16, name="junk")
+        d_v = [const.tile([P, 4], F32, name="d_v%d" % g) for g in range(G)]
+        r_v = [const.tile([P, 4], F32, name="r_v%d" % g) for g in range(G)]
+        d_p = [const.tile([P, 4], F32, name="d_p%d" % g) for g in range(G)]
+        e_p = [const.tile([P, 4], F32, name="e_p%d" % g) for g in range(G)]
+        r_p = [const.tile([P, 4], F32, name="r_p%d" % g) for g in range(G)]
+
+        def load_adj(g, r0, r1):
+            nc.sync.dma_start(out=adj_sb[g][:, r0 * N : r1 * N], in_=adj_v[g, :, r0 * N : r1 * N])
+
+        def load_x(g, k0, k1):
+            nc.sync.dma_start(
+                out=x_sb[g][:, k0 * N : k1 * N].rearrange("p (k f) -> p k f", f=N),
+                in_=x_v[g, :, k0:k1, :],
+            )
+
+        load_x(0, 0, 2)
+        load_x(0, 2, 4)
+        load_adj(0, 0, 2)
+        load_adj(0, 2, 4)
+        nc.sync.dma_start(
+            out=w_sb[:].rearrange("p (t e) -> p t e", t=4),
+            in_=w.rearrange("(t p) e -> p t e", p=P),
+        )
+        load_adj(0, 4, 6)
+        load_x(1, 0, 4)
+        load_adj(0, 6, 8)
+        load_adj(1, 0, 4)
+        load_adj(1, 4, 8)
+        load_x(2, 0, 4)
+        load_adj(2, 0, 8)
+        load_x(3, 0, 4)
+        load_adj(3, 0, 8)
+
+        nc.vector.memset(zb[:], 0.0)
+        nc.vector.memset(ones[:], 1.0)
+        nc.scalar.dma_start(out=zb[0:1, :], in_=b.rearrange("(o n) -> o n", o=1))
+        make_identity(nc, identf[:])
+        make_identity(nc, identb[:])
+
+        st = {}
+
+        def regroup(dst, src):
+            nc.vector.tensor_copy(
+                out=dst.rearrange("p (c i t) -> p c t i", i=4, t=4),
+                in_=src.rearrange("p (t c i) -> p c t i", t=4, i=4),
+            )
+
+        def xr(g, c):
+            if c == 0:
+                st["xg", g] = two.tile([P, 4 * N], BF16, name="xg%d" % g, tag="xg", align_bytes=64)
+            regroup(st["xg", g][:, c * 2048 : (c + 1) * 2048], x_sb[g][:, c * 2048 : (c + 1) * 2048])
+
+        def xq(g, c0, c1):
+            if c0 == 0:
+                st["xc", g] = two.tile([P, N], U32, name="xc%d" % g, tag="xc", align_bytes=64)
+                st["xs", g] = two.tile([P, N], U8, name="xs%d" % g, tag="xs", align_bytes=64)
+            nc.vector.quantize_mx(
+                out=st["xc", g][:, c0 * D : c1 * D].bitcast(FP8X4),
+                scales=st["xs", g][:, c0 * D : c1 * D],
+                in_=st["xg", g][:, c0 * 2048 : c1 * 2048],
+            )
+
+        def t_(n):
+            g, r = divmod(n, R)
+            tp = ps_tp.tile([P, 512], F32, name="tp%d" % n, tag="tp")
+            st["tp", n] = tp
+            for k in range(4):
+                nc.tensor.transpose(
+                    out=tp[:, k * P : (k + 1) * P],
+                    in_=adj_w[g][:, r * 512 + k * P : r * 512 + (k + 1) * P],
+                    identity=identf[:],
+                )
+
+        def a_(n):
+            gt = four.tile([P, N], BF16, name="gt%d" % n, tag="gt", align_bytes=64)
+            st["gt", n] = gt
+            nc.scalar.copy(
+                out=gt[:].bitcast(F32).rearrange("p (c i u) -> p c i u", c=2, u=2),
+                in_=st["tp", n][:].rearrange("p (c u i) -> p c i u", c=2, u=2),
+            )
+
+        def qa(n):
+            ac = four.tile([P, 256], U32, name="ac%d" % n, tag="ac", align_bytes=64)
+            sc = four.tile([P, 256], U8, name="as%d" % n, tag="as", align_bytes=64)
+            st["ac", n] = ac
+            st["as", n] = sc
+            nc.vector.quantize_mx(out=ac[:].bitcast(FP8X4), scales=sc[:], in_=st["gt", n][:])
+
+        def m1(n):
+            g = n // R
+            p1 = ps_p1.tile([P, 512], F32, name="p1_%d" % n, tag="p1")
+            st["p1", n] = p1
+            for t in range(4):
+                for c in range(2):
+                    lo = c * D + t * P
+                    nc.tensor.matmul_mx(
+                        out=p1[:, t * P : (t + 1) * P],
+                        lhsT=st["xc", g][:, lo : lo + P].bitcast(FP8X4),
+                        lhsT_scale=st["xs", g][:, lo : lo + P],
+                        rhs=st["ac", n][:, c * P : (c + 1) * P].bitcast(FP8X4),
+                        rhs_scale=st["as", n][:, c * P : (c + 1) * P],
+                        start=(c == 0),
+                        stop=(c == 1),
+                    )
+
+        def b_(n):
+            g2 = four.tile([P, D], BF16, name="g2_%d" % n, tag="g2", align_bytes=64)
+            st["g2", n] = g2
+            dst = g2[:].rearrange("p (i t) -> p i t", t=4)
+            src = st["p1", n][:].rearrange("p (t i) -> p i t", t=4)
+            if n in B_ON_V:
+                nc.vector.tensor_copy(out=dst, in_=src)
+            else:
+                nc.scalar.copy(out=dst, in_=src)
+
+        def qb(n):
+            c2 = four.tile([P, P], U32, name="bc%d" % n, tag="bc", align_bytes=64)
+            s2 = four.tile([P, P], U8, name="bs%d" % n, tag="bs", align_bytes=64)
+            st["bc", n] = c2
+            st["bs", n] = s2
+            nc.vector.quantize_mx(out=c2[:].bitcast(FP8X4), scales=s2[:], in_=st["g2", n][:])
+
+        def m2(n):
+            p2 = ps_p2.tile([P, D], F32, name="p2_%d" % n, tag="p2")
+            st["p2", n] = p2
+            nc.tensor.matmul_mx(
+                out=p2[:],
+                lhsT=st["bc", n][:].bitcast(FP8X4),
+                lhsT_scale=st["bs", n][:],
+                rhs=wc[:].bitcast(FP8X4),
+                rhs_scale=ws[:],
+                start=True,
+                stop=True,
+            )
+
+        def c1(n):
+            z = four.tile([P, D], F32, name="z%d" % n, tag="z")
+            st["z", n] = z
+            nc.vector.tensor_tensor(out=z[:], in0=st["p2", n][:], in1=bb[:], op=ALU.add)
+
+        def c2(n):
+            g, r = divmod(n, R)
+            if n % 2 == 0:
+                st["o", n // 2] = six.tile([P, 2 * D], F32, name="o%d" % (n // 2), tag="o")
+            o = st["o", n // 2][:, (n % 2) * D : (n % 2 + 1) * D]
+            rd = r_v[g][:, r : r + 1] if r < 4 else r_p[g][:, r - 4 : r - 3]
+            if n in C2_ON_V:
+                nc.vector.tensor_scalar(
+                    out=o, in0=st["z", n][:], scalar1=rd, scalar2=0.0, op0=ALU.mult, op1=ALU.max
+                )
+            else:
+                nc.scalar.activation(out=o, in_=st["z", n][:], func=ACT.Relu, scale=rd)
+
+        def store(m):
+            g, k = divmod(m, R // 2)
+            nc.sync.dma_start(out=out_v[g, :, 2 * k * D : (2 * k + 2) * D], in_=st["o", m][:])
+
+        def dnv(g, r):
+            nc.vector.tensor_scalar(
+                out=junk[:],
+                in0=adj_sb[g][:, r * N : (r + 1) * N],
+                scalar1=1.0,
+                scalar2=1.0,
+                op0=ALU.mult,
+                op1=ALU.add,
+                accum_out=d_v[g][:, r : r + 1],
+            )
+
+        def rcv(g):
+            nc.vector.reciprocal(out=r_v[g][:], in_=d_v[g][:])
+
+        def fold(g, k):
+            if k == 0:
+                st["pd", g] = ps_pd.tile([P, 512], F32, name="pd%d" % g, tag="pd")
+            r = 4 + k
+            for q in range(8):
+                nc.tensor.matmul(
+                    out=st["pd", g][:, k * P : (k + 1) * P],
+                    lhsT=identb[:],
+                    rhs=adj_sb[g][:, r * N + q * P : r * N + (q + 1) * P],
+                    start=(q == 0),
+                    stop=(q == 7),
+                )
+
+        def fred(g):
+            nc.vector.tensor_reduce(
+                out=d_p[g][:],
+                in_=st["pd", g][:].rearrange("p (k n) -> p k n", k=4),
+                axis=AX.X,
+                op=ALU.add,
+            )
+            nc.vector.tensor_scalar_add(out=e_p[g][:], in0=d_p[g][:], scalar1=1.0)
+            nc.vector.reciprocal(out=r_p[g][:], in_=e_p[g][:])
+
+        def pair(m):
+            return [2 * m, 2 * m + 1] if 0 <= m < NPAIR else []
+
+        xr(0, 0)
+        xr(0, 1)
+        xq(0, 0, 1)
+        xq(0, 1, 2)
+        pb = ps_p2.tile([P, D], F32, name="pb", tag="p2")
+        nc.tensor.matmul(out=pb[:], lhsT=ones[:], rhs=zb[:], start=True, stop=True)
+        nc.scalar.copy(out=bb[:], in_=pb[:])
+        for n in pair(0):
+            t_(n)
+
+        for s in range(NPAIR + 2):
+            g, q = divmod(s, 4)
+            for n in pair(s - 2):
+                c1(n)
+            for n in pair(s):
+                a_(n)
+            if 1 <= s <= NPAIR:
+                fold((s - 1) // 4, (s - 1) % 4)
+            for n in pair(s + 1):
+                t_(n)
+            for n in pair(s):
+                qa(n)
+            for n in pair(s - 1):
+                b_(n)
+            for n in pair(s):
+                m1(n)
+            if s == 0:
+                regroup(wg[:], w_sb[:])
+            if q == 0 and g >= 1:
+                fred(g - 1)
+            if g + 1 < G:
+                if q == 1:
+                    xr(g + 1, 0)
+                if q == 2:
+                    xr(g + 1, 1)
+                if q == 3:
+                    xq(g + 1, 0, 2)
+            for n in pair(s - 1):
+                qb(n)
+            for n in pair(s - 1):
+                m2(n)
+            for n in pair(s - 2):
+                c2(n)
+            if 0 <= s - 2 < NPAIR:
+                store(s - 2)
+            if s == 0:
+                nc.vector.quantize_mx(out=wc[:].bitcast(FP8X4), scales=ws[:], in_=wg[:])
+                dnv(0, 0)
+            if s == 1:
+                dnv(0, 1)
+            k = s + 2
+            if k < NPAIR:
+                dnv(k // 4, k % 4)
+                if k % 4 == 3:
+                    rcv(k // 4)

@@ -22,7 +22,7 @@ NPAIR = NU // 2
 FLOPS = 2 * G * N * N * D + 2 * G * N * D * D
 
 MANUAL = True
-C2_ON_V = ()
+C2_ON_V = tuple(range(1, NU, 2))
 B_ON_V = ()
 
 
@@ -54,14 +54,9 @@ def tile_msamodel_pa_kernel(tc, x, adj, w, b, out):
         zb = const.tile([P, D], BF16, name="zb")
         ones = const.tile([P, P], BF16, name="ones")
         identf = const.tile([P, P], F32, name="identf")
-        identb = const.tile([P, P], BF16, name="identb")
         bb = const.tile([P, D], F32, name="bb")
-        junk = const.tile([P, N], BF16, name="junk")
-        d_v = [const.tile([P, 4], F32, name="d_v%d" % g) for g in range(G)]
-        r_v = [const.tile([P, 4], F32, name="r_v%d" % g) for g in range(G)]
-        d_p = [const.tile([P, 4], F32, name="d_p%d" % g) for g in range(G)]
-        e_p = [const.tile([P, 4], F32, name="e_p%d" % g) for g in range(G)]
-        r_p = [const.tile([P, 4], F32, name="r_p%d" % g) for g in range(G)]
+        e_t = [const.tile([P, 4], F32, name="e_t%d" % k) for k in range(NU // 4)]
+        r_t = [const.tile([P, 4], F32, name="r_t%d" % k) for k in range(NU // 4)]
 
         def load_adj(g, r0, r1):
             nc.sync.dma_start(out=adj_sb[g][:, r0 * N : r1 * N], in_=adj_v[g, :, r0 * N : r1 * N])
@@ -94,7 +89,6 @@ def tile_msamodel_pa_kernel(tc, x, adj, w, b, out):
         nc.vector.memset(ones[:], 1.0)
         nc.scalar.dma_start(out=zb[0:1, :], in_=b.rearrange("(o n) -> o n", o=1))
         make_identity(nc, identf[:])
-        make_identity(nc, identb[:])
 
         st = {}
 
@@ -198,11 +192,10 @@ def tile_msamodel_pa_kernel(tc, x, adj, w, b, out):
             nc.vector.tensor_tensor(out=z[:], in0=st["p2", n][:], in1=bb[:], op=ALU.add)
 
         def c2(n):
-            g, r = divmod(n, R)
-            if n % 2 == 0:
+            if ("o", n // 2) not in st:
                 st["o", n // 2] = six.tile([P, 2 * D], F32, name="o%d" % (n // 2), tag="o")
             o = st["o", n // 2][:, (n % 2) * D : (n % 2 + 1) * D]
-            rd = r_v[g][:, r : r + 1] if r < 4 else r_p[g][:, r - 4 : r - 3]
+            rd = r_t[n // 4][:, n % 4 : n % 4 + 1]
             if n in C2_ON_V:
                 nc.vector.tensor_scalar(
                     out=o, in0=st["z", n][:], scalar1=rd, scalar2=0.0, op0=ALU.mult, op1=ALU.max
@@ -214,42 +207,22 @@ def tile_msamodel_pa_kernel(tc, x, adj, w, b, out):
             g, k = divmod(m, R // 2)
             nc.sync.dma_start(out=out_v[g, :, 2 * k * D : (2 * k + 2) * D], in_=st["o", m][:])
 
-        def dnv(g, r):
-            nc.vector.tensor_scalar(
-                out=junk[:],
-                in0=adj_sb[g][:, r * N : (r + 1) * N],
-                scalar1=1.0,
-                scalar2=1.0,
-                op0=ALU.mult,
-                op1=ALU.add,
-                accum_out=d_v[g][:, r : r + 1],
-            )
-
-        def rcv(g):
-            nc.vector.reciprocal(out=r_v[g][:], in_=d_v[g][:])
-
-        def fold(g, k):
-            if k == 0:
-                st["pd", g] = ps_pd.tile([P, 512], F32, name="pd%d" % g, tag="pd")
-            r = 4 + k
-            for q in range(8):
+        def dn(n):
+            if n % 4 == 0:
+                st["pd", n // 4] = ps_pd.tile([P, 4], F32, name="pd%d" % (n // 4), tag="pd")
+            cols = st["gt", n][:].rearrange("p (c i t) -> p c t i", c=2, t=4)
+            for k in range(8):
                 nc.tensor.matmul(
-                    out=st["pd", g][:, k * P : (k + 1) * P],
-                    lhsT=identb[:],
-                    rhs=adj_sb[g][:, r * N + q * P : r * N + (q + 1) * P],
-                    start=(q == 0),
-                    stop=(q == 7),
+                    out=st["pd", n // 4][:, n % 4 : n % 4 + 1],
+                    lhsT=cols[:, k // 4, k % 4, :],
+                    rhs=ones[:, 0:1],
+                    start=(k == 0),
+                    stop=(k == 7),
                 )
 
-        def fred(g):
-            nc.vector.tensor_reduce(
-                out=d_p[g][:],
-                in_=st["pd", g][:].rearrange("p (k n) -> p k n", k=4),
-                axis=AX.X,
-                op=ALU.add,
-            )
-            nc.vector.tensor_scalar_add(out=e_p[g][:], in0=d_p[g][:], scalar1=1.0)
-            nc.vector.reciprocal(out=r_p[g][:], in_=e_p[g][:])
+        def rb(k):
+            nc.vector.tensor_scalar_add(out=e_t[k][:], in0=st["pd", k][:], scalar1=1.0)
+            nc.vector.reciprocal(out=r_t[k][:], in_=e_t[k][:])
 
         def pair(m):
             return [2 * m, 2 * m + 1] if 0 <= m < NPAIR else []
@@ -258,54 +231,50 @@ def tile_msamodel_pa_kernel(tc, x, adj, w, b, out):
         xr(0, 1)
         xq(0, 0, 1)
         xq(0, 1, 2)
-        pb = ps_p2.tile([P, D], F32, name="pb", tag="p2")
-        nc.tensor.matmul(out=pb[:], lhsT=ones[:], rhs=zb[:], start=True, stop=True)
-        nc.scalar.copy(out=bb[:], in_=pb[:])
-        for n in pair(0):
-            t_(n)
 
-        for s in range(NPAIR + 2):
+        for s in range(-1, NPAIR + 3):
             g, q = divmod(s, 4)
-            for n in pair(s - 2):
-                c1(n)
+            if s == 2:
+                nc.scalar.copy(out=bb[:], in_=st["pb"][:])
             for n in pair(s):
                 a_(n)
-            if 1 <= s <= NPAIR:
-                fold((s - 1) // 4, (s - 1) % 4)
+            for n in pair(s):
+                dn(n)
+            if s == 1:
+                st["pb"] = ps_p2.tile([P, D], F32, name="pb", tag="p2")
+                nc.tensor.matmul(out=st["pb"][:], lhsT=ones[:], rhs=zb[:], start=True, stop=True)
             for n in pair(s + 1):
                 t_(n)
+            for n in pair(s - 2):
+                m2(n)
             for n in pair(s):
                 qa(n)
+            if 0 <= s < NPAIR and s % 2 == 1:
+                rb(s // 2)
             for n in pair(s - 1):
                 b_(n)
             for n in pair(s):
                 m1(n)
             if s == 0:
                 regroup(wg[:], w_sb[:])
-            if q == 0 and g >= 1:
-                fred(g - 1)
-            if g + 1 < G:
+            if s >= 0 and g + 1 < G:
                 if q == 1:
                     xr(g + 1, 0)
                 if q == 2:
                     xr(g + 1, 1)
                 if q == 3:
                     xq(g + 1, 0, 2)
+            if s == 1:
+                nc.vector.quantize_mx(out=wc[:].bitcast(FP8X4), scales=ws[:], in_=wg[:])
+            for n in pair(s - 3):
+                if n in C2_ON_V:
+                    c2(n)
             for n in pair(s - 1):
                 qb(n)
-            for n in pair(s - 1):
-                m2(n)
             for n in pair(s - 2):
-                c2(n)
-            if 0 <= s - 2 < NPAIR:
-                store(s - 2)
-            if s == 0:
-                nc.vector.quantize_mx(out=wc[:].bitcast(FP8X4), scales=ws[:], in_=wg[:])
-                dnv(0, 0)
-            if s == 1:
-                dnv(0, 1)
-            k = s + 2
-            if k < NPAIR:
-                dnv(k // 4, k % 4)
-                if k % 4 == 3:
-                    rcv(k // 4)
+                c1(n)
+            for n in pair(s - 3):
+                if n not in C2_ON_V:
+                    c2(n)
+            if 0 <= s - 3 < NPAIR:
+                store(s - 3)

@@ -22,7 +22,7 @@ NPAIR = NU // 2
 FLOPS = 2 * G * N * N * D + 2 * G * N * D * D
 
 MANUAL = True
-C2_ON_V = tuple(range(1, NU, 2))
+C2_ON_V = tuple(range(1, NU, 3))
 B_ON_V = ()
 
 
@@ -34,9 +34,10 @@ def tile_msamodel_pa_kernel(tc, x, adj, w, b, out):
         four = ctx.enter_context(tc.tile_pool(name="four", bufs=4))
         six = ctx.enter_context(tc.tile_pool(name="six", bufs=6))
         ps_tp = ctx.enter_context(tc.psum_pool(name="ps_tp", bufs=2))
-        ps_p1 = ctx.enter_context(tc.psum_pool(name="ps_p1", bufs=3))
+        ps_p1 = ctx.enter_context(tc.psum_pool(name="ps_p1", bufs=2))
         ps_p2 = ctx.enter_context(tc.psum_pool(name="ps_p2", bufs=2))
         ps_pd = ctx.enter_context(tc.psum_pool(name="ps_pd", bufs=1))
+        ps_dn = ctx.enter_context(tc.psum_pool(name="ps_dn", bufs=1))
         if MANUAL:
             ctx.enter_context(tc.manual_schedule())
 
@@ -55,6 +56,8 @@ def tile_msamodel_pa_kernel(tc, x, adj, w, b, out):
         ones = const.tile([P, P], BF16, name="ones")
         identf = const.tile([P, P], F32, name="identf")
         bb = const.tile([P, D], F32, name="bb")
+        qf = const.tile([P, 32], F32, name="qf")
+        sel = const.tile([P, 4 * P], BF16, name="sel")
         e_t = [const.tile([P, 4], F32, name="e_t%d" % k) for k in range(NU // 4)]
         r_t = [const.tile([P, 4], F32, name="r_t%d" % k) for k in range(NU // 4)]
 
@@ -89,6 +92,12 @@ def tile_msamodel_pa_kernel(tc, x, adj, w, b, out):
         nc.vector.memset(ones[:], 1.0)
         nc.scalar.dma_start(out=zb[0:1, :], in_=b.rearrange("(o n) -> o n", o=1))
         make_identity(nc, identf[:])
+        nc.vector.memset(sel[:], 0.0)
+        nc.vector.tensor_reduce(
+            out=qf[:], in_=identf[:].rearrange("p (j t) -> p j t", t=4), axis=AX.X, op=ALU.add
+        )
+        for ib in range(4):
+            nc.vector.tensor_copy(out=sel[:, ib * P + 32 * ib : ib * P + 32 * ib + 32], in_=qf[:])
 
         st = {}
 
@@ -209,19 +218,44 @@ def tile_msamodel_pa_kernel(tc, x, adj, w, b, out):
 
         def dn(n):
             if n % 4 == 0:
-                st["pd", n // 4] = ps_pd.tile([P, 4], F32, name="pd%d" % (n // 4), tag="pd")
-            cols = st["gt", n][:].rearrange("p (c i t) -> p c t i", c=2, t=4)
-            for k in range(8):
+                st["pd", n // 4] = ps_pd.tile([P, 16], F32, name="pd%d" % (n // 4), tag="pd")
+            for ib in range(4):
+                for c in range(2):
+                    nc.tensor.matmul(
+                        out=st["pd", n // 4][:, ib * 4 + n % 4 : ib * 4 + n % 4 + 1],
+                        lhsT=st["gt", n][:, c * D + ib * P : c * D + (ib + 1) * P],
+                        rhs=ones[:, 0:1],
+                        start=(c == 0),
+                        stop=(c == 1),
+                    )
+
+        def split(k):
+            p32 = two.tile([P, 16], F32, name="p32_%d" % k, tag="p32")
+            hi = two.tile([P, 16], BF16, name="hi%d" % k, tag="hi")
+            r1 = two.tile([P, 16], F32, name="r1_%d" % k, tag="r1")
+            mid = two.tile([P, 16], BF16, name="mid%d" % k, tag="mid")
+            lo = two.tile([P, 16], BF16, name="lo%d" % k, tag="lo")
+            st["terms", k] = (hi, mid, lo)
+            nc.scalar.copy(out=p32[:], in_=st["pd", k][:])
+            nc.scalar.copy(out=hi[:], in_=st["pd", k][:])
+            nc.gpsimd.tensor_tensor(out=r1[:], in0=p32[:], in1=hi[:], op=ALU.subtract)
+            nc.gpsimd.tensor_scalar(out=mid[:], in0=r1[:], scalar1=1.0, scalar2=0.0, op0=ALU.mult, op1=ALU.add)
+            nc.gpsimd.tensor_tensor(out=lo[:], in0=r1[:], in1=mid[:], op=ALU.subtract)
+
+        def gather(k):
+            den = ps_dn.tile([P, 4], F32, name="den%d" % k, tag="den")
+            st["den", k] = den
+            for j in range(12):
                 nc.tensor.matmul(
-                    out=st["pd", n // 4][:, n % 4 : n % 4 + 1],
-                    lhsT=cols[:, k // 4, k % 4, :],
-                    rhs=ones[:, 0:1],
-                    start=(k == 0),
-                    stop=(k == 7),
+                    out=den[:],
+                    lhsT=sel[:, (j % 4) * P : (j % 4 + 1) * P],
+                    rhs=st["terms", k][j // 4][:, (j % 4) * 4 : (j % 4 + 1) * 4],
+                    start=(j == 0),
+                    stop=(j == 11),
                 )
 
         def rb(k):
-            nc.vector.tensor_scalar_add(out=e_t[k][:], in0=st["pd", k][:], scalar1=1.0)
+            nc.vector.tensor_scalar_add(out=e_t[k][:], in0=st["den", k][:], scalar1=1.0)
             nc.vector.reciprocal(out=r_t[k][:], in_=e_t[k][:])
 
         def pair(m):
@@ -234,6 +268,9 @@ def tile_msamodel_pa_kernel(tc, x, adj, w, b, out):
 
         for s in range(-1, NPAIR + 3):
             g, q = divmod(s, 4)
+            batch = (s - 2) // 2 if (2 <= s <= NPAIR and s % 2 == 0) else None
+            if batch is not None:
+                split(batch)
             if s == 2:
                 nc.scalar.copy(out=bb[:], in_=st["pb"][:])
             for n in pair(s):
@@ -245,12 +282,12 @@ def tile_msamodel_pa_kernel(tc, x, adj, w, b, out):
                 nc.tensor.matmul(out=st["pb"][:], lhsT=ones[:], rhs=zb[:], start=True, stop=True)
             for n in pair(s + 1):
                 t_(n)
+            if batch is not None:
+                gather(batch)
             for n in pair(s - 2):
                 m2(n)
             for n in pair(s):
                 qa(n)
-            if 0 <= s < NPAIR and s % 2 == 1:
-                rb(s // 2)
             for n in pair(s - 1):
                 b_(n)
             for n in pair(s):
@@ -266,6 +303,8 @@ def tile_msamodel_pa_kernel(tc, x, adj, w, b, out):
                     xq(g + 1, 0, 2)
             if s == 1:
                 nc.vector.quantize_mx(out=wc[:].bitcast(FP8X4), scales=ws[:], in_=wg[:])
+            if batch is not None:
+                rb(batch)
             for n in pair(s - 3):
                 if n in C2_ON_V:
                     c2(n)

@@ -31,13 +31,12 @@ def tile_msamodel_pa_kernel(tc, x, adj, w, b, out):
     with ExitStack() as ctx:
         const = ctx.enter_context(tc.tile_pool(name="const", bufs=1))
         two = ctx.enter_context(tc.tile_pool(name="two", bufs=2))
-        four = ctx.enter_context(tc.tile_pool(name="four", bufs=4))
+        four = ctx.enter_context(tc.tile_pool(name="four", bufs=6))
         six = ctx.enter_context(tc.tile_pool(name="six", bufs=6))
         ps_tp = ctx.enter_context(tc.psum_pool(name="ps_tp", bufs=2))
-        ps_p1 = ctx.enter_context(tc.psum_pool(name="ps_p1", bufs=2))
+        ps_p1 = ctx.enter_context(tc.psum_pool(name="ps_p1", bufs=3))
         ps_p2 = ctx.enter_context(tc.psum_pool(name="ps_p2", bufs=2))
         ps_pd = ctx.enter_context(tc.psum_pool(name="ps_pd", bufs=1))
-        ps_dn = ctx.enter_context(tc.psum_pool(name="ps_dn", bufs=1))
         if MANUAL:
             ctx.enter_context(tc.manual_schedule())
 
@@ -56,8 +55,6 @@ def tile_msamodel_pa_kernel(tc, x, adj, w, b, out):
         ones = const.tile([P, P], BF16, name="ones")
         identf = const.tile([P, P], F32, name="identf")
         bb = const.tile([P, D], F32, name="bb")
-        qf = const.tile([P, 32], F32, name="qf")
-        sel = const.tile([P, 4 * P], BF16, name="sel")
         e_t = [const.tile([P, 4], F32, name="e_t%d" % k) for k in range(NU // 4)]
         r_t = [const.tile([P, 4], F32, name="r_t%d" % k) for k in range(NU // 4)]
 
@@ -71,8 +68,9 @@ def tile_msamodel_pa_kernel(tc, x, adj, w, b, out):
             )
 
         load_x(0, 0, 2)
+        load_adj(0, 0, 1)
         load_x(0, 2, 4)
-        load_adj(0, 0, 2)
+        load_adj(0, 1, 2)
         load_adj(0, 2, 4)
         nc.sync.dma_start(
             out=w_sb[:].rearrange("p (t e) -> p t e", t=4),
@@ -92,12 +90,6 @@ def tile_msamodel_pa_kernel(tc, x, adj, w, b, out):
         nc.vector.memset(ones[:], 1.0)
         nc.scalar.dma_start(out=zb[0:1, :], in_=b.rearrange("(o n) -> o n", o=1))
         make_identity(nc, identf[:])
-        nc.vector.memset(sel[:], 0.0)
-        nc.vector.tensor_reduce(
-            out=qf[:], in_=identf[:].rearrange("p (j t) -> p j t", t=4), axis=AX.X, op=ALU.add
-        )
-        for ib in range(4):
-            nc.vector.tensor_copy(out=sel[:, ib * P + 32 * ib : ib * P + 32 * ib + 32], in_=qf[:])
 
         st = {}
 
@@ -212,50 +204,27 @@ def tile_msamodel_pa_kernel(tc, x, adj, w, b, out):
             else:
                 nc.scalar.activation(out=o, in_=st["z", n][:], func=ACT.Relu, scale=rd)
 
-        def store(m):
+        def store(m, u0, u1):
             g, k = divmod(m, R // 2)
-            nc.sync.dma_start(out=out_v[g, :, 2 * k * D : (2 * k + 2) * D], in_=st["o", m][:])
+            nc.sync.dma_start(
+                out=out_v[g, :, (2 * k + u0) * D : (2 * k + u1) * D], in_=st["o", m][:, u0 * D : u1 * D]
+            )
 
         def dn(n):
             if n % 4 == 0:
-                st["pd", n // 4] = ps_pd.tile([P, 16], F32, name="pd%d" % (n // 4), tag="pd")
-            for ib in range(4):
-                for c in range(2):
-                    nc.tensor.matmul(
-                        out=st["pd", n // 4][:, ib * 4 + n % 4 : ib * 4 + n % 4 + 1],
-                        lhsT=st["gt", n][:, c * D + ib * P : c * D + (ib + 1) * P],
-                        rhs=ones[:, 0:1],
-                        start=(c == 0),
-                        stop=(c == 1),
-                    )
-
-        def split(k):
-            p32 = two.tile([P, 16], F32, name="p32_%d" % k, tag="p32")
-            hi = two.tile([P, 16], BF16, name="hi%d" % k, tag="hi")
-            r1 = two.tile([P, 16], F32, name="r1_%d" % k, tag="r1")
-            mid = two.tile([P, 16], BF16, name="mid%d" % k, tag="mid")
-            lo = two.tile([P, 16], BF16, name="lo%d" % k, tag="lo")
-            st["terms", k] = (hi, mid, lo)
-            nc.scalar.copy(out=p32[:], in_=st["pd", k][:])
-            nc.scalar.copy(out=hi[:], in_=st["pd", k][:])
-            nc.gpsimd.tensor_tensor(out=r1[:], in0=p32[:], in1=hi[:], op=ALU.subtract)
-            nc.gpsimd.tensor_scalar(out=mid[:], in0=r1[:], scalar1=1.0, scalar2=0.0, op0=ALU.mult, op1=ALU.add)
-            nc.gpsimd.tensor_tensor(out=lo[:], in0=r1[:], in1=mid[:], op=ALU.subtract)
-
-        def gather(k):
-            den = ps_dn.tile([P, 4], F32, name="den%d" % k, tag="den")
-            st["den", k] = den
-            for j in range(12):
+                st["pd", n // 4] = ps_pd.tile([P, 4], F32, name="pd%d" % (n // 4), tag="pd")
+            cols = st["gt", n][:].rearrange("p (c i t) -> p c t i", c=2, t=4)
+            for k in range(8):
                 nc.tensor.matmul(
-                    out=den[:],
-                    lhsT=sel[:, (j % 4) * P : (j % 4 + 1) * P],
-                    rhs=st["terms", k][j // 4][:, (j % 4) * 4 : (j % 4 + 1) * 4],
-                    start=(j == 0),
-                    stop=(j == 11),
+                    out=st["pd", n // 4][:, n % 4 : n % 4 + 1],
+                    lhsT=cols[:, k // 4, k % 4, :],
+                    rhs=ones[:, 0:1],
+                    start=(k == 0),
+                    stop=(k == 7),
                 )
 
         def rb(k):
-            nc.vector.tensor_scalar_add(out=e_t[k][:], in0=st["den", k][:], scalar1=1.0)
+            nc.vector.tensor_scalar_add(out=e_t[k][:], in0=st["pd", k][:], scalar1=1.0)
             nc.vector.reciprocal(out=r_t[k][:], in_=e_t[k][:])
 
         def pair(m):
@@ -268,9 +237,6 @@ def tile_msamodel_pa_kernel(tc, x, adj, w, b, out):
 
         for s in range(-1, NPAIR + 3):
             g, q = divmod(s, 4)
-            batch = (s - 2) // 2 if (2 <= s <= NPAIR and s % 2 == 0) else None
-            if batch is not None:
-                split(batch)
             if s == 2:
                 nc.scalar.copy(out=bb[:], in_=st["pb"][:])
             for n in pair(s):
@@ -282,12 +248,12 @@ def tile_msamodel_pa_kernel(tc, x, adj, w, b, out):
                 nc.tensor.matmul(out=st["pb"][:], lhsT=ones[:], rhs=zb[:], start=True, stop=True)
             for n in pair(s + 1):
                 t_(n)
-            if batch is not None:
-                gather(batch)
             for n in pair(s - 2):
                 m2(n)
             for n in pair(s):
                 qa(n)
+            if 0 <= s < NPAIR and s % 2 == 1:
+                rb(s // 2)
             for n in pair(s - 1):
                 b_(n)
             for n in pair(s):
@@ -303,11 +269,11 @@ def tile_msamodel_pa_kernel(tc, x, adj, w, b, out):
                     xq(g + 1, 0, 2)
             if s == 1:
                 nc.vector.quantize_mx(out=wc[:].bitcast(FP8X4), scales=ws[:], in_=wg[:])
-            if batch is not None:
-                rb(batch)
             for n in pair(s - 3):
                 if n in C2_ON_V:
                     c2(n)
+                    if s - 3 == NPAIR - 1:
+                        store(s - 3, n % 2, n % 2 + 1)
             for n in pair(s - 1):
                 qb(n)
             for n in pair(s - 2):
@@ -315,5 +281,7 @@ def tile_msamodel_pa_kernel(tc, x, adj, w, b, out):
             for n in pair(s - 3):
                 if n not in C2_ON_V:
                     c2(n)
-            if 0 <= s - 3 < NPAIR:
-                store(s - 3)
+                    if s - 3 == NPAIR - 1:
+                        store(s - 3, n % 2, n % 2 + 1)
+            if 0 <= s - 3 < NPAIR - 1:
+                store(s - 3, 0, 2)

@@ -241,7 +241,7 @@ def tile_msamodel_pa_kernel(tc, x, adj, w, b, out):
                 nc.scalar.copy(out=bb[:], in_=st["pb"][:])
             for n in pair(s):
                 a_(n)
-            for n in pair(s):
+            for n in pair(s - 1):
                 dn(n)
             if s == 1:
                 st["pb"] = ps_p2.tile([P, D], F32, name="pb", tag="p2")
@@ -252,8 +252,6 @@ def tile_msamodel_pa_kernel(tc, x, adj, w, b, out):
                 m2(n)
             for n in pair(s):
                 qa(n)
-            if 0 <= s < NPAIR and s % 2 == 1:
-                rb(s // 2)
             for n in pair(s - 1):
                 b_(n)
             for n in pair(s):
@@ -269,6 +267,8 @@ def tile_msamodel_pa_kernel(tc, x, adj, w, b, out):
                     xq(g + 1, 0, 2)
             if s == 1:
                 nc.vector.quantize_mx(out=wc[:].bitcast(FP8X4), scales=ws[:], in_=wg[:])
+            if 2 <= s <= NPAIR and s % 2 == 0:
+                rb((s - 2) // 2)
             for n in pair(s - 3):
                 if n in C2_ON_V:
                     c2(n)

from contextlib import ExitStack

import concourse.mybir as mybir
from concourse.masks import make_identity

F32 = mybir.dt.float32
BF16 = mybir.dt.bfloat16
U32 = mybir.dt.uint32
U8 = mybir.dt.uint8
FP8X4 = mybir.dt.float8_e4m3fn_x4
ALU = mybir.AluOpType
ACT = mybir.ActivationFunctionType
AX = mybir.AxisListType

G = 4
N = 1024
D = 512
P = 128
R = N // P
NU = G * R
NPAIR = NU // 2
FLOPS = 2 * G * N * N * D + 2 * G * N * D * D

MANUAL = True
C2_ON_V = tuple(range(1, NU, 3))
B_ON_V = ()


def tile_msamodel_pa_kernel(tc, x, adj, w, b, out):
    nc = tc.nc
    with ExitStack() as ctx:
        const = ctx.enter_context(tc.tile_pool(name="const", bufs=1))
        two = ctx.enter_context(tc.tile_pool(name="two", bufs=2))
        four = ctx.enter_context(tc.tile_pool(name="four", bufs=6))
        six = ctx.enter_context(tc.tile_pool(name="six", bufs=6))
        ps_tp = ctx.enter_context(tc.psum_pool(name="ps_tp", bufs=2))
        ps_p1 = ctx.enter_context(tc.psum_pool(name="ps_p1", bufs=3))
        ps_p2 = ctx.enter_context(tc.psum_pool(name="ps_p2", bufs=2))
        ps_pd = ctx.enter_context(tc.psum_pool(name="ps_pd", bufs=1))
        if MANUAL:
            ctx.enter_context(tc.manual_schedule())

        adj_v = adj.rearrange("g (p r) j -> g p (r j)", r=R)
        x_v = x.rearrange("g (k p e) d -> g p k (e d)", k=4, p=P, e=2)
        out_v = out.rearrange("g (p r) e -> g p (r e)", r=R)

        adj_sb = [const.tile([P, R * N], BF16, name="adj%d" % g) for g in range(G)]
        adj_w = [t[:].bitcast(F32) for t in adj_sb]
        x_sb = [const.tile([P, 4 * N], BF16, name="x%d" % g) for g in range(G)]
        w_sb = const.tile([P, 4 * D], BF16, name="w_sb")
        wg = const.tile([P, 4 * D], BF16, name="wg", align_bytes=64)
        wc = const.tile([P, D], U32, name="wc", align_bytes=64)
        ws = const.tile([P, D], U8, name="ws", align_bytes=64)
        zb = const.tile([P, D], BF16, name="zb")
        ones = const.tile([P, P], BF16, name="ones")
        identf = const.tile([P, P], F32, name="identf")
        bb = const.tile([P, D], F32, name="bb")
        e_t = [const.tile([P, 4], F32, name="e_t%d" % k) for k in range(NU // 4)]
        r_t = [const.tile([P, 4], F32, name="r_t%d" % k) for k in range(NU // 4)]

        def load_adj(g, r0, r1):
            nc.sync.dma_start(out=adj_sb[g][:, r0 * N : r1 * N], in_=adj_v[g, :, r0 * N : r1 * N])

        def load_x(g, k0, k1):
            nc.sync.dma_start(
                out=x_sb[g][:, k0 * N : k1 * N].rearrange("p (k f) -> p k f", f=N),
                in_=x_v[g, :, k0:k1, :],
            )

        load_x(0, 0, 2)
        load_adj(0, 0, 1)
        load_x(0, 2, 4)
        load_adj(0, 1, 2)
        load_adj(0, 2, 4)
        nc.sync.dma_start(
            out=w_sb[:].rearrange("p (t e) -> p t e", t=4),
            in_=w.rearrange("(t p) e -> p t e", p=P),
        )
        load_adj(0, 4, 6)
        load_x(1, 0, 4)
        load_adj(0, 6, 8)
        load_adj(1, 0, 4)
        load_adj(1, 4, 8)
        load_x(2, 0, 4)
        load_adj(2, 0, 8)
        load_x(3, 0, 4)
        load_adj(3, 0, 8)

        nc.vector.memset(zb[:], 0.0)
        nc.vector.memset(ones[:], 1.0)
        nc.scalar.dma_start(out=zb[0:1, :], in_=b.rearrange("(o n) -> o n", o=1))
        make_identity(nc, identf[:])

        st = {}

        def regroup(dst, src):
            nc.vector.tensor_copy(
                out=dst.rearrange("p (c i t) -> p c t i", i=4, t=4),
                in_=src.rearrange("p (t c i) -> p c t i", t=4, i=4),
            )

        def xr(g, c):
            if c == 0:
                st["xg", g] = two.tile([P, 4 * N], BF16, name="xg%d" % g, tag="xg", align_bytes=64)
            regroup(st["xg", g][:, c * 2048 : (c + 1) * 2048], x_sb[g][:, c * 2048 : (c + 1) * 2048])

        def xq(g, c0, c1):
            if c0 == 0:
                st["xc", g] = two.tile([P, N], U32, name="xc%d" % g, tag="xc", align_bytes=64)
                st["xs", g] = two.tile([P, N], U8, name="xs%d" % g, tag="xs", align_bytes=64)
            nc.vector.quantize_mx(
                out=st["xc", g][:, c0 * D : c1 * D].bitcast(FP8X4),
                scales=st["xs", g][:, c0 * D : c1 * D],
                in_=st["xg", g][:, c0 * 2048 : c1 * 2048],
            )

        def t_(n):
            g, r = divmod(n, R)
            tp = ps_tp.tile([P, 512], F32, name="tp%d" % n, tag="tp")
            st["tp", n] = tp
            for k in range(4):
                nc.tensor.transpose(
                    out=tp[:, k * P : (k + 1) * P],
                    in_=adj_w[g][:, r * 512 + k * P : r * 512 + (k + 1) * P],
                    identity=identf[:],
                )

        def a_(n):
            gt = four.tile([P, N], BF16, name="gt%d" % n, tag="gt", align_bytes=64)
            st["gt", n] = gt
            nc.scalar.copy(
                out=gt[:].bitcast(F32).rearrange("p (c i u) -> p c i u", c=2, u=2),
                in_=st["tp", n][:].rearrange("p (c u i) -> p c i u", c=2, u=2),
            )

        def qa(n):
            ac = four.tile([P, 256], U32, name="ac%d" % n, tag="ac", align_bytes=64)
            sc = four.tile([P, 256], U8, name="as%d" % n, tag="as", align_bytes=64)
            st["ac", n] = ac
            st["as", n] = sc
            nc.vector.quantize_mx(out=ac[:].bitcast(FP8X4), scales=sc[:], in_=st["gt", n][:])

        def m1(n):
            g = n // R
            p1 = ps_p1.tile([P, 512], F32, name="p1_%d" % n, tag="p1")
            st["p1", n] = p1
            for t in range(4):
                for c in range(2):
                    lo = c * D + t * P
                    nc.tensor.matmul_mx(
                        out=p1[:, t * P : (t + 1) * P],
                        lhsT=st["xc", g][:, lo : lo + P].bitcast(FP8X4),
                        lhsT_scale=st["xs", g][:, lo : lo + P],
                        rhs=st["ac", n][:, c * P : (c + 1) * P].bitcast(FP8X4),
                        rhs_scale=st["as", n][:, c * P : (c + 1) * P],
                        start=(c == 0),
                        stop=(c == 1),
                    )

        def b_(n):
            g2 = four.tile([P, D], BF16, name="g2_%d" % n, tag="g2", align_bytes=64)
            st["g2", n] = g2
            dst = g2[:].rearrange("p (i t) -> p i t", t=4)
            src = st["p1", n][:].rearrange("p (t i) -> p i t", t=4)
            if n in B_ON_V:
                nc.vector.tensor_copy(out=dst, in_=src)
            else:
                nc.scalar.copy(out=dst, in_=src)

        def qb(n):
            c2 = four.tile([P, P], U32, name="bc%d" % n, tag="bc", align_bytes=64)
            s2 = four.tile([P, P], U8, name="bs%d" % n, tag="bs", align_bytes=64)
            st["bc", n] = c2
            st["bs", n] = s2
            nc.vector.quantize_mx(out=c2[:].bitcast(FP8X4), scales=s2[:], in_=st["g2", n][:])

        def m2(n):
            p2 = ps_p2.tile([P, D], F32, name="p2_%d" % n, tag="p2")
            st["p2", n] = p2
            nc.tensor.matmul_mx(
                out=p2[:],
                lhsT=st["bc", n][:].bitcast(FP8X4),
                lhsT_scale=st["bs", n][:],
                rhs=wc[:].bitcast(FP8X4),
                rhs_scale=ws[:],
                start=True,
                stop=True,
            )

        def c1(n):
            z = four.tile([P, D], F32, name="z%d" % n, tag="z")
            st["z", n] = z
            nc.vector.tensor_tensor(out=z[:], in0=st["p2", n][:], in1=bb[:], op=ALU.add)

        def c2(n):
            if ("o", n // 2) not in st:
                st["o", n // 2] = six.tile([P, 2 * D], F32, name="o%d" % (n // 2), tag="o")
            o = st["o", n // 2][:, (n % 2) * D : (n % 2 + 1) * D]
            rd = r_t[n // 4][:, n % 4 : n % 4 + 1]
            if n in C2_ON_V:
                nc.vector.tensor_scalar(
                    out=o, in0=st["z", n][:], scalar1=rd, scalar2=0.0, op0=ALU.mult, op1=ALU.max
                )
            else:
                nc.scalar.activation(out=o, in_=st["z", n][:], func=ACT.Relu, scale=rd)

        def store(m, u0, u1):
            g, k = divmod(m, R // 2)
            nc.sync.dma_start(
                out=out_v[g, :, (2 * k + u0) * D : (2 * k + u1) * D], in_=st["o", m][:, u0 * D : u1 * D]
            )

        def dn(n):
            if n % 4 == 0:
                st["pd", n // 4] = ps_pd.tile([P, 4], F32, name="pd%d" % (n // 4), tag="pd")
            cols = st["gt", n][:].rearrange("p (c i t) -> p c t i", c=2, t=4)
            for k in range(8):
                nc.tensor.matmul(
                    out=st["pd", n // 4][:, n % 4 : n % 4 + 1],
                    lhsT=cols[:, k // 4, k % 4, :],
                    rhs=ones[:, 0:1],
                    start=(k == 0),
                    stop=(k == 7),
                )

        def rb(k):
            nc.vector.tensor_scalar_add(out=e_t[k][:], in0=st["pd", k][:], scalar1=1.0)
            nc.vector.reciprocal(out=r_t[k][:], in_=e_t[k][:])

        def pair(m):
            return [2 * m, 2 * m + 1] if 0 <= m < NPAIR else []

        xr(0, 0)
        xr(0, 1)
        xq(0, 0, 1)
        xq(0, 1, 2)

        for s in range(-1, NPAIR + 3):
            g, q = divmod(s, 4)
            if s == 2:
                nc.scalar.copy(out=bb[:], in_=st["pb"][:])
            for n in pair(s):
                a_(n)
            for n in pair(s - 1):
                dn(n)
            if s == 1:
                st["pb"] = ps_p2.tile([P, D], F32, name="pb", tag="p2")
                nc.tensor.matmul(out=st["pb"][:], lhsT=ones[:], rhs=zb[:], start=True, stop=True)
            for n in pair(s + 1):
                t_(n)
            for n in pair(s - 2):
                m2(n)
            for n in pair(s):
                qa(n)
            for n in pair(s - 1):
                b_(n)
            for n in pair(s):
                m1(n)
            if s == 0:
                regroup(wg[:], w_sb[:])
            if s >= 0 and g + 1 < G:
                if q == 1:
                    xr(g + 1, 0)
                if q == 2:
                    xr(g + 1, 1)
                if q == 3:
                    xq(g + 1, 0, 2)
            if s == 1:
                nc.vector.quantize_mx(out=wc[:].bitcast(FP8X4), scales=ws[:], in_=wg[:])
            if 2 <= s <= NPAIR and s % 2 == 0:
                rb((s - 2) // 2)
            for n in pair(s - 3):
                if n in C2_ON_V:
                    c2(n)
                    if s - 3 == NPAIR - 1:
                        store(s - 3, n % 2, n % 2 + 1)
            for n in pair(s - 1):
                qb(n)
            for n in pair(s - 2):
                c1(n)
            for n in pair(s - 3):
                if n not in C2_ON_V:
                    c2(n)
                    if s - 3 == NPAIR - 1:
                        store(s - 3, n % 2, n % 2 + 1)
            if 0 <= s - 3 < NPAIR - 1:
                store(s - 3, 0, 2)
